import numpy as np
import ml_dtypes


def mxq(x, axis, fmt="e4m3"):
    dtype, down = {"e4m3": (ml_dtypes.float8_e4m3fn, 7), "e5m2": (ml_dtypes.float8_e5m2, 14)}[fmt]
    v = np.moveaxis(np.asarray(x, np.float32).astype(ml_dtypes.bfloat16).astype(np.float64), axis, -1)
    blocks = v.reshape(v.shape[:-1] + (-1, 32))
    amax = np.abs(blocks).max(-1, keepdims=True)
    byte = np.maximum(np.where(amax > 0, np.frexp(amax)[1] - 1 + 127, 0) - down, 1)
    scale = np.exp2(byte - 127.0)
    codes = (blocks / scale).astype(np.float32).astype(dtype).astype(np.float64)
    return np.moveaxis((codes * scale).reshape(v.shape), -1, axis)


WIDE = False


def mx_kscale(k):
    if not WIDE:
        return np.ones(k)
    levels = np.array([10, -10, 5, -5, 0])
    a = np.random.permutation(np.resize(levels, k // 512 * 4)).reshape(k // 512, 4)
    idx = np.arange(k)
    return np.exp2(a[idx // 512, idx % 128 // 32])


BF16 = ml_dtypes.bfloat16


def bf(x):
    return np.asarray(x, np.float32).astype(BF16)


def f64(x):
    return np.asarray(x).astype(np.float64)


B, V, K, C = 2, 4096, 512, 512


def setup_inputs():
    s = mx_kscale(K)
    u = np.exp2(np.round(np.log2(s / s.max()) / 2))
    return {"evals": bf(np.random.uniform(0.0, 4.0, (B, K)) + np.log(u * u)),
            "evecs": bf(np.random.standard_normal((B, V, K)) * 2.0 / np.sqrt(K) * u),
            "count": C}


def reference(evals, evecs, count):
    scales = 10.0 ** np.linspace(-2.0, 0.0, count)
    coefs = np.exp(-f64(evals)[:, None, :] * scales[None, :, None])
    ev = f64(evecs)
    sq = ev * ev
    return mxq(sq, 2, "e4m3") @ mxq(coefs, 2, "e4m3").transpose(0, 2, 1)

@@ -1,0 +1,184 @@
+from contextlib import ExitStack
+
+import concourse.mybir as mybir
+from concourse.masks import make_identity
+
+F32 = mybir.dt.float32
+BF16 = mybir.dt.bfloat16
+U32 = mybir.dt.uint32
+U8 = mybir.dt.uint8
+FP8X4 = mybir.dt.float8_e4m3fn_x4
+ACT = mybir.ActivationFunctionType
+ALU = mybir.AluOpType
+
+P = 128
+B, V, K, C = 2, 4096, 512, 512
+TILES = V // P
+GROUPS = [4] * 15 + [2, 2]
+NG = len(GROUPS)
+FIRST = [sum(GROUPS[:g]) for g in range(NG)]
+
+FLOPS = 2 * B * V * K * C
+
+LOADS = [(0, 0, 2), (0, 2, 2), (0, 4, 4), (0, 8, 8), (0, 16, 16), (1, 0, 32)]
+STAGE_BUFS = 10
+SCALAR_COPIES = [0, 1, 0, 0, 1, 0, 0, 1, 0, 0, 1, 0, 1, 1, 2, 1, 1]
+EXP1_AFTER = 3
+
+
+def tile_hks_t_kernel(tc, evals, evecs, count, out):
+    nc = tc.nc
+    assert tuple(evecs.shape) == (B, V, K) and count == C
+
+    with ExitStack() as ctx:
+        consts = ctx.enter_context(tc.tile_pool(name="consts", bufs=1))
+        xpool = ctx.enter_context(tc.tile_pool(name="xpool", bufs=1))
+        gpool = ctx.enter_context(tc.tile_pool(name="gpool", bufs=3))
+        spool = ctx.enter_context(tc.tile_pool(name="spool", bufs=STAGE_BUFS))
+        psum = ctx.enter_context(tc.psum_pool(name="psum", bufs=4))
+        ctx.enter_context(tc.manual_schedule())
+
+        ev = consts.tile([P, 4 * B], BF16, name="ev")
+        with nc.allow_non_contiguous_dma(reason="evals: two neighbouring values to a partition"):
+            nc.sync.dma_start(
+                out=ev[:].rearrange("p (b u e) -> p b u e", b=B, u=2, e=2),
+                in_=evals.rearrange("b (u p e) -> p b u e", u=2, p=P, e=2),
+            )
+        words = {}
+        for b, t0, n in LOADS:
+            x = xpool.tile([P, n * K], BF16, name="x_%d_%d" % (b, t0))
+            src = evecs[b].rearrange("(p t) k -> p (t k)", t=TILES)
+            nc.sync.dma_start(out=x[:], in_=src[:, t0 * K : (t0 + n) * K])
+            xw = x[:].bitcast(F32)
+            for j in range(n):
+                words[b * TILES + t0 + j] = xw[:, j * (K // 2) : (j + 1) * (K // 2)]
+
+        ident = consts.tile([P, P], F32, name="ident")
+        make_identity(nc, ident[:])
+
+        powers = consts.tile([P, C], F32, name="powers")
+        nc.vector.memset(powers[:, 0:1], 1.0)
+        warm = consts.tile([P, 1], F32, name="warm")
+        nc.scalar.activation(out=warm[:], in_=powers[:, 0:1], func=ACT.Exp)
+        n = 1
+        while n < C:
+            nc.vector.tensor_scalar(
+                out=powers[:, n : 2 * n],
+                in0=powers[:, 0:n],
+                scalar1=10.0 ** (2.0 * n / (C - 1)),
+                scalar2=None,
+                op0=ALU.mult,
+            )
+            n *= 2
+
+        args = {}
+        coef_codes = {}
+        coef_scales = {}
+
+        def coef_args(b):
+            a = consts.tile([P, 4 * C], F32, name="arg%d" % b)
+            nc.vector.tensor_tensor(
+                out=a[:].rearrange("p (c t) -> p c t", t=4),
+                in0=powers[:].unsqueeze(2).to_broadcast([P, C, 4]),
+                in1=ev[:, 4 * b : 4 * b + 4].unsqueeze(1).to_broadcast([P, C, 4]),
+                op=ALU.mult,
+            )
+            args[b] = a
+
+        def coef_exp(b):
+            cf = consts.tile([P, 4 * C], BF16, name="cf%d" % b, align_bytes=64)
+            nc.scalar.activation(out=cf[:], in_=args[b][:], func=ACT.Exp, scale=-0.01)
+            args[b] = cf
+
+        def coef_quant(b):
+            cc = consts.tile([P, C], U32, name="cc%d" % b, align_bytes=64)
+            cs = consts.tile([P, C], U8, name="cs%d" % b, align_bytes=64)
+            nc.vector.quantize_mx(out=cc[:].bitcast(FP8X4), scales=cs[:], in_=args[b][:])
+            coef_codes[b] = cc
+            coef_scales[b] = cs
+
+        banks = {}
+        grouped = {}
+        codes = {}
+        scales = {}
+        accs = {}
+
+        def transposes(g):
+            banks[g] = []
+            for h in range(GROUPS[g] // 2):
+                xt = psum.tile([P, 512], F32, name="xt", tag="xt")
+                for vt in range(2):
+                    src = words[FIRST[g] + 2 * h + vt]
+                    for u in range(2):
+                        lo = u * 256 + vt * P
+                        nc.tensor.transpose(xt[:, lo : lo + P], src[:, u * P : (u + 1) * P], ident[:])
+                banks[g].append(xt)
+
+        def squares(g):
+            grp = gpool.tile([P, GROUPS[g] * K], BF16, name="grouped", tag="grouped", align_bytes=64)
+            for h in range(GROUPS[g] // 2):
+                nc.scalar.activation(
+                    out=grp[:, h * 1024 : (h + 1) * 1024].rearrange("p (c u e) -> p c u e", u=2, e=2),
+                    in_=banks[g][h][:].bitcast(BF16).rearrange("p (u c e) -> p c u e", u=2, e=2),
+                    func=ACT.Square,
+                )
+            grouped[g] = grp
+
+        def quantise(g):
+            cd = gpool.tile([P, GROUPS[g] * P], U32, name="codes", tag="codes", align_bytes=64)
+            sc = gpool.tile([P, GROUPS[g] * P], U8, name="scales", tag="scales", align_bytes=64)
+            nc.vector.quantize_mx(out=cd[:].bitcast(FP8X4), scales=sc[:], in_=grouped[g][:])
+            codes[g] = cd
+            scales[g] = sc
+
+        def multiply(g):
+            b = FIRST[g] // TILES
+            accs[g] = []
+            for j in range(GROUPS[g]):
+                acc = psum.tile([P, C], F32, name="acc", tag="acc")
+                nc.tensor.matmul_mx(
+                    out=acc[:],
+                    lhsT=codes[g][:, j * P : (j + 1) * P].bitcast(FP8X4),
+                    lhsT_scale=scales[g][:, j * P : (j + 1) * P],
+                    rhs=coef_codes[b][:].bitcast(FP8X4),
+                    rhs_scale=coef_scales[b][:],
+                    start=True,
+                    stop=True,
+                )
+                accs[g].append(acc)
+
+        def copy_out(g):
+            b = FIRST[g] // TILES
+            t0 = FIRST[g] % TILES
+            stage = spool.tile([P, GROUPS[g] * C], F32, name="stage", tag="stage")
+            for j in range(GROUPS[g]):
+                dst = stage[:, j * C : (j + 1) * C]
+                if j < SCALAR_COPIES[g]:
+                    nc.scalar.copy(out=dst, in_=accs[g][j][:])
+                else:
+                    nc.vector.tensor_copy(out=dst, in_=accs[g][j][:])
+            dram = out[b].rearrange("(p t) c -> p (t c)", t=TILES)
+            nc.sync.dma_start(out=dram[:, t0 * C : (t0 + GROUPS[g]) * C], in_=stage[:])
+
+        coef_args(0)
+        coef_args(1)
+        transposes(0)
+        transposes(1)
+        squares(0)
+        coef_exp(0)
+        for g in range(NG):
+            quantise(g)
+            if g == 0:
+                coef_quant(0)
+            if g == EXP1_AFTER + 1:
+                coef_quant(1)
+            if g + 2 < NG:
+                transposes(g + 2)
+            if g > 0:
+                copy_out(g - 1)
+            if g + 1 < NG:
+                squares(g + 1)
+            if g == EXP1_AFTER:
+                coef_exp(1)
+            multiply(g)
+        copy_out(NG - 1)

@@ -22,8 +22,9 @@ FLOPS = 2 * B * V * K * C
 
 LOADS = [(0, 0, 2), (0, 2, 2), (0, 4, 4), (0, 8, 8), (0, 16, 16), (1, 0, 32)]
 STAGE_BUFS = 10
-SCALAR_COPIES = [0, 1, 0, 0, 1, 0, 0, 1, 0, 0, 1, 0, 1, 1, 2, 1, 1]
+SCALAR_COPIES = [0, 0, 0, 0, 0, 0, 1, 0, 1, 0, 1, 0, 1, 1, 2, 1, 1]
 EXP1_AFTER = 3
+QUANT1_AT = 5
 
 
 def tile_hks_t_kernel(tc, evals, evecs, count, out):
@@ -147,16 +148,20 @@ def tile_hks_t_kernel(tc, evals, evecs, count, out):
                 )
                 accs[g].append(acc)
 
-        def copy_out(g):
+        stages = {}
+
+        def vector_copies(g):
+            stage = spool.tile([P, GROUPS[g] * C], F32, name="stage", tag="stage")
+            for j in range(GROUPS[g] - SCALAR_COPIES[g]):
+                nc.vector.tensor_copy(out=stage[:, j * C : (j + 1) * C], in_=accs[g][j][:])
+            stages[g] = stage
+
+        def scalar_copies_and_store(g):
             b = FIRST[g] // TILES
             t0 = FIRST[g] % TILES
-            stage = spool.tile([P, GROUPS[g] * C], F32, name="stage", tag="stage")
-            for j in range(GROUPS[g]):
-                dst = stage[:, j * C : (j + 1) * C]
-                if j < SCALAR_COPIES[g]:
-                    nc.scalar.copy(out=dst, in_=accs[g][j][:])
-                else:
-                    nc.vector.tensor_copy(out=dst, in_=accs[g][j][:])
+            stage = stages[g]
+            for j in range(GROUPS[g] - SCALAR_COPIES[g], GROUPS[g]):
+                nc.scalar.copy(out=stage[:, j * C : (j + 1) * C], in_=accs[g][j][:])
             dram = out[b].rearrange("(p t) c -> p (t c)", t=TILES)
             nc.sync.dma_start(out=dram[:, t0 * C : (t0 + GROUPS[g]) * C], in_=stage[:])
 
@@ -170,15 +175,18 @@ def tile_hks_t_kernel(tc, evals, evecs, count, out):
             quantise(g)
             if g == 0:
                 coef_quant(0)
-            if g == EXP1_AFTER + 1:
-                coef_quant(1)
             if g + 2 < NG:
                 transposes(g + 2)
             if g > 0:
-                copy_out(g - 1)
+                vector_copies(g - 1)
+            if g == QUANT1_AT:
+                coef_quant(1)
             if g + 1 < NG:
                 squares(g + 1)
+            if g > 0:
+                scalar_copies_and_store(g - 1)
             if g == EXP1_AFTER:
                 coef_exp(1)
             multiply(g)
-        copy_out(NG - 1)
+        vector_copies(NG - 1)
+        scalar_copies_and_store(NG - 1)

@@ -14,17 +14,24 @@ ALU = mybir.AluOpType
 P = 128
 B, V, K, C = 2, 4096, 512, 512
 TILES = V // P
-GROUPS = [4] * 15 + [2, 2]
-NG = len(GROUPS)
-FIRST = [sum(GROUPS[:g]) for g in range(NG)]
+PAIR = 2
+STEPS = B * TILES // PAIR
 
 FLOPS = 2 * B * V * K * C
 
 LOADS = [(0, 0, 2), (0, 2, 2), (0, 4, 4), (0, 8, 8), (0, 16, 16), (1, 0, 32)]
+STORES = [4] * 15 + [2, 2]
+STORE_FIRST = [sum(STORES[:s]) for s in range(len(STORES))]
+STORE_OF = [s for s in range(len(STORES)) for i in range(STORES[s])]
 STAGE_BUFS = 10
-SCALAR_COPIES = [0, 0, 0, 0, 0, 0, 1, 0, 1, 0, 1, 0, 1, 1, 2, 1, 1]
-EXP1_AFTER = 3
-QUANT1_AT = 5
+T_AHEAD = 4
+SQ_AHEAD = 2
+EXP1_AT = 7
+QUANT1_AT = 10
+
+
+def scalar_copies_second(g):
+    return (g >= 12 and g % 4 == 0) or g >= STEPS - 4
 
 
 def tile_hks_t_kernel(tc, evals, evecs, count, out):
@@ -34,7 +41,7 @@ def tile_hks_t_kernel(tc, evals, evecs, count, out):
     with ExitStack() as ctx:
         consts = ctx.enter_context(tc.tile_pool(name="consts", bufs=1))
         xpool = ctx.enter_context(tc.tile_pool(name="xpool", bufs=1))
-        gpool = ctx.enter_context(tc.tile_pool(name="gpool", bufs=3))
+        gpool = ctx.enter_context(tc.tile_pool(name="gpool", bufs=4))
         spool = ctx.enter_context(tc.tile_pool(name="spool", bufs=STAGE_BUFS))
         psum = ctx.enter_context(tc.psum_pool(name="psum", bufs=4))
         ctx.enter_context(tc.manual_schedule())
@@ -73,72 +80,65 @@ def tile_hks_t_kernel(tc, evals, evecs, count, out):
             n *= 2
 
         args = {}
+        coefs = {}
         coef_codes = {}
         coef_scales = {}
 
         def coef_args(b):
-            a = consts.tile([P, 4 * C], F32, name="arg%d" % b)
+            args[b] = consts.tile([P, 4 * C], F32, name="arg%d" % b)
             nc.vector.tensor_tensor(
-                out=a[:].rearrange("p (c t) -> p c t", t=4),
+                out=args[b][:].rearrange("p (c t) -> p c t", t=4),
                 in0=powers[:].unsqueeze(2).to_broadcast([P, C, 4]),
                 in1=ev[:, 4 * b : 4 * b + 4].unsqueeze(1).to_broadcast([P, C, 4]),
                 op=ALU.mult,
             )
-            args[b] = a
 
         def coef_exp(b):
-            cf = consts.tile([P, 4 * C], BF16, name="cf%d" % b, align_bytes=64)
-            nc.scalar.activation(out=cf[:], in_=args[b][:], func=ACT.Exp, scale=-0.01)
-            args[b] = cf
+            coefs[b] = consts.tile([P, 4 * C], BF16, name="cf%d" % b, align_bytes=64)
+            nc.scalar.activation(out=coefs[b][:], in_=args[b][:], func=ACT.Exp, scale=-0.01)
 
         def coef_quant(b):
-            cc = consts.tile([P, C], U32, name="cc%d" % b, align_bytes=64)
-            cs = consts.tile([P, C], U8, name="cs%d" % b, align_bytes=64)
-            nc.vector.quantize_mx(out=cc[:].bitcast(FP8X4), scales=cs[:], in_=args[b][:])
-            coef_codes[b] = cc
-            coef_scales[b] = cs
+            coef_codes[b] = consts.tile([P, C], U32, name="cc%d" % b, align_bytes=64)
+            coef_scales[b] = consts.tile([P, C], U8, name="cs%d" % b, align_bytes=64)
+            nc.vector.quantize_mx(
+                out=coef_codes[b][:].bitcast(FP8X4), scales=coef_scales[b][:], in_=coefs[b][:]
+            )
 
         banks = {}
         grouped = {}
         codes = {}
         scales = {}
         accs = {}
+        stages = {}
 
         def transposes(g):
-            banks[g] = []
-            for h in range(GROUPS[g] // 2):
-                xt = psum.tile([P, 512], F32, name="xt", tag="xt")
-                for vt in range(2):
-                    src = words[FIRST[g] + 2 * h + vt]
-                    for u in range(2):
-                        lo = u * 256 + vt * P
-                        nc.tensor.transpose(xt[:, lo : lo + P], src[:, u * P : (u + 1) * P], ident[:])
-                banks[g].append(xt)
+            banks[g] = psum.tile([P, 512], F32, name="xt", tag="xt")
+            for vt in range(PAIR):
+                for u in range(2):
+                    lo = u * PAIR * P + vt * P
+                    nc.tensor.transpose(
+                        banks[g][:, lo : lo + P], words[PAIR * g + vt][:, u * P : (u + 1) * P], ident[:]
+                    )
 
         def squares(g):
-            grp = gpool.tile([P, GROUPS[g] * K], BF16, name="grouped", tag="grouped", align_bytes=64)
-            for h in range(GROUPS[g] // 2):
-                nc.scalar.activation(
-                    out=grp[:, h * 1024 : (h + 1) * 1024].rearrange("p (c u e) -> p c u e", u=2, e=2),
-                    in_=banks[g][h][:].bitcast(BF16).rearrange("p (u c e) -> p c u e", u=2, e=2),
-                    func=ACT.Square,
-                )
-            grouped[g] = grp
+            grouped[g] = gpool.tile([P, PAIR * K], BF16, name="grouped", tag="grouped", align_bytes=64)
+            nc.scalar.activation(
+                out=grouped[g][:].rearrange("p (c u e) -> p c u e", u=2, e=2),
+                in_=banks[g][:].bitcast(BF16).rearrange("p (u c e) -> p c u e", u=2, e=2),
+                func=ACT.Square,
+            )
 
         def quantise(g):
-            cd = gpool.tile([P, GROUPS[g] * P], U32, name="codes", tag="codes", align_bytes=64)
-            sc = gpool.tile([P, GROUPS[g] * P], U8, name="scales", tag="scales", align_bytes=64)
-            nc.vector.quantize_mx(out=cd[:].bitcast(FP8X4), scales=sc[:], in_=grouped[g][:])
-            codes[g] = cd
-            scales[g] = sc
+            codes[g] = gpool.tile([P, PAIR * P], U32, name="codes", tag="codes", align_bytes=64)
+            scales[g] = gpool.tile([P, PAIR * P], U8, name="scales", tag="scales", align_bytes=64)
+            nc.vector.quantize_mx(out=codes[g][:].bitcast(FP8X4), scales=scales[g][:], in_=grouped[g][:])
 
         def multiply(g):
-            b = FIRST[g] // TILES
-            accs[g] = []
-            for j in range(GROUPS[g]):
-                acc = psum.tile([P, C], F32, name="acc", tag="acc")
+            b = PAIR * g // TILES
+            for j in range(PAIR):
+                accs[PAIR * g + j] = psum.tile([P, C], F32, name="acc", tag="acc")
                 nc.tensor.matmul_mx(
-                    out=acc[:],
+                    out=accs[PAIR * g + j][:],
                     lhsT=codes[g][:, j * P : (j + 1) * P].bitcast(FP8X4),
                     lhsT_scale=scales[g][:, j * P : (j + 1) * P],
                     rhs=coef_codes[b][:].bitcast(FP8X4),
@@ -146,47 +146,52 @@ def tile_hks_t_kernel(tc, evals, evecs, count, out):
                     start=True,
                     stop=True,
                 )
-                accs[g].append(acc)
 
-        stages = {}
+        def copy_out(i, on_scalar):
+            s = STORE_OF[i]
+            if i == STORE_FIRST[s]:
+                stages[s] = spool.tile([P, STORES[s] * C], F32, name="stage", tag="stage")
+            lo = (i - STORE_FIRST[s]) * C
+            if on_scalar:
+                nc.scalar.copy(out=stages[s][:, lo : lo + C], in_=accs[i][:])
+            else:
+                nc.vector.tensor_copy(out=stages[s][:, lo : lo + C], in_=accs[i][:])
 
-        def vector_copies(g):
-            stage = spool.tile([P, GROUPS[g] * C], F32, name="stage", tag="stage")
-            for j in range(GROUPS[g] - SCALAR_COPIES[g]):
-                nc.vector.tensor_copy(out=stage[:, j * C : (j + 1) * C], in_=accs[g][j][:])
-            stages[g] = stage
-
-        def scalar_copies_and_store(g):
-            b = FIRST[g] // TILES
-            t0 = FIRST[g] % TILES
-            stage = stages[g]
-            for j in range(GROUPS[g] - SCALAR_COPIES[g], GROUPS[g]):
-                nc.scalar.copy(out=stage[:, j * C : (j + 1) * C], in_=accs[g][j][:])
-            dram = out[b].rearrange("(p t) c -> p (t c)", t=TILES)
-            nc.sync.dma_start(out=dram[:, t0 * C : (t0 + GROUPS[g]) * C], in_=stage[:])
+        def store_if_full(i):
+            s = STORE_OF[i]
+            if i + 1 == STORE_FIRST[s] + STORES[s]:
+                b = i // TILES
+                t0 = STORE_FIRST[s] % TILES
+                dram = out[b].rearrange("(p t) c -> p (t c)", t=TILES)
+                nc.sync.dma_start(out=dram[:, t0 * C : (t0 + STORES[s]) * C], in_=stages[s][:])
 
         coef_args(0)
         coef_args(1)
-        transposes(0)
-        transposes(1)
+        for g in range(T_AHEAD):
+            transposes(g)
         squares(0)
         coef_exp(0)
-        for g in range(NG):
-            quantise(g)
+        squares(1)
+        for g in range(STEPS + 1):
+            if g < STEPS:
+                quantise(g)
             if g == 0:
                 coef_quant(0)
-            if g + 2 < NG:
-                transposes(g + 2)
+            if g + T_AHEAD < STEPS:
+                transposes(g + T_AHEAD)
             if g > 0:
-                vector_copies(g - 1)
+                copy_out(PAIR * (g - 1), False)
+                if not scalar_copies_second(g - 1):
+                    copy_out(PAIR * (g - 1) + 1, False)
             if g == QUANT1_AT:
                 coef_quant(1)
-            if g + 1 < NG:
-                squares(g + 1)
+            if g + SQ_AHEAD < STEPS:
+                squares(g + SQ_AHEAD)
             if g > 0:
-                scalar_copies_and_store(g - 1)
-            if g == EXP1_AFTER:
+                if scalar_copies_second(g - 1):
+                    copy_out(PAIR * (g - 1) + 1, True)
+                store_if_full(PAIR * (g - 1) + 1)
+            if g == EXP1_AT:
                 coef_exp(1)
-            multiply(g)
-        vector_copies(NG - 1)
-        scalar_copies_and_store(NG - 1)
+            if g < STEPS:
+                multiply(g)

@@ -14,24 +14,17 @@ ALU = mybir.AluOpType
 P = 128
 B, V, K, C = 2, 4096, 512, 512
 TILES = V // P
-PAIR = 2
-STEPS = B * TILES // PAIR
+GROUPS = [4] * 15 + [2, 2]
+NG = len(GROUPS)
+FIRST = [sum(GROUPS[:g]) for g in range(NG)]
 
 FLOPS = 2 * B * V * K * C
 
 LOADS = [(0, 0, 2), (0, 2, 2), (0, 4, 4), (0, 8, 8), (0, 16, 16), (1, 0, 32)]
-STORES = [4] * 15 + [2, 2]
-STORE_FIRST = [sum(STORES[:s]) for s in range(len(STORES))]
-STORE_OF = [s for s in range(len(STORES)) for i in range(STORES[s])]
 STAGE_BUFS = 10
-T_AHEAD = 4
-SQ_AHEAD = 2
-EXP1_AT = 7
-QUANT1_AT = 10
-
-
-def scalar_copies_second(g):
-    return (g >= 12 and g % 4 == 0) or g >= STEPS - 4
+SCALAR_COPIES = [0, 0, 1, 0, 1, 0, 1, 0, 1, 0, 1, 0, 1, 1, 2, 1, 1]
+EXP1_AFTER = 3
+QUANT1_AT = 5
 
 
 def tile_hks_t_kernel(tc, evals, evecs, count, out):
@@ -41,7 +34,7 @@ def tile_hks_t_kernel(tc, evals, evecs, count, out):
     with ExitStack() as ctx:
         consts = ctx.enter_context(tc.tile_pool(name="consts", bufs=1))
         xpool = ctx.enter_context(tc.tile_pool(name="xpool", bufs=1))
-        gpool = ctx.enter_context(tc.tile_pool(name="gpool", bufs=4))
+        gpool = ctx.enter_context(tc.tile_pool(name="gpool", bufs=3))
         spool = ctx.enter_context(tc.tile_pool(name="spool", bufs=STAGE_BUFS))
         psum = ctx.enter_context(tc.psum_pool(name="psum", bufs=4))
         ctx.enter_context(tc.manual_schedule())
@@ -80,65 +73,83 @@ def tile_hks_t_kernel(tc, evals, evecs, count, out):
             n *= 2
 
         args = {}
-        coefs = {}
         coef_codes = {}
         coef_scales = {}
 
         def coef_args(b):
-            args[b] = consts.tile([P, 4 * C], F32, name="arg%d" % b)
+            a = consts.tile([P, 4 * C], F32, name="arg%d" % b)
             nc.vector.tensor_tensor(
-                out=args[b][:].rearrange("p (c t) -> p c t", t=4),
+                out=a[:].rearrange("p (c t) -> p c t", t=4),
                 in0=powers[:].unsqueeze(2).to_broadcast([P, C, 4]),
                 in1=ev[:, 4 * b : 4 * b + 4].unsqueeze(1).to_broadcast([P, C, 4]),
                 op=ALU.mult,
             )
+            args[b] = a
 
         def coef_exp(b):
-            coefs[b] = consts.tile([P, 4 * C], BF16, name="cf%d" % b, align_bytes=64)
-            nc.scalar.activation(out=coefs[b][:], in_=args[b][:], func=ACT.Exp, scale=-0.01)
+            cf = consts.tile([P, 4 * C], BF16, name="cf%d" % b, align_bytes=64)
+            nc.scalar.activation(out=cf[:], in_=args[b][:], func=ACT.Exp, scale=-0.01)
+            args[b] = cf
 
         def coef_quant(b):
-            coef_codes[b] = consts.tile([P, C], U32, name="cc%d" % b, align_bytes=64)
-            coef_scales[b] = consts.tile([P, C], U8, name="cs%d" % b, align_bytes=64)
-            nc.vector.quantize_mx(
-                out=coef_codes[b][:].bitcast(FP8X4), scales=coef_scales[b][:], in_=coefs[b][:]
-            )
+            cc = consts.tile([P, C], U32, name="cc%d" % b, align_bytes=64)
+            cs = consts.tile([P, C], U8, name="cs%d" % b, align_bytes=64)
+            nc.vector.quantize_mx(out=cc[:].bitcast(FP8X4), scales=cs[:], in_=args[b][:])
+            coef_codes[b] = cc
+            coef_scales[b] = cs
 
         banks = {}
         grouped = {}
         codes = {}
         scales = {}
         accs = {}
-        stages = {}
 
         def transposes(g):
-            banks[g] = psum.tile([P, 512], F32, name="xt", tag="xt")
-            for vt in range(PAIR):
-                for u in range(2):
-                    lo = u * PAIR * P + vt * P
-                    nc.tensor.transpose(
-                        banks[g][:, lo : lo + P], words[PAIR * g + vt][:, u * P : (u + 1) * P], ident[:]
-                    )
+            banks[g] = []
+            for h in range(GROUPS[g] // 2):
+                xt = psum.tile([P, 512], F32, name="xt", tag="xt")
+                for vt in range(2):
+                    src = words[FIRST[g] + 2 * h + vt]
+                    for u in range(2):
+                        lo = u * 256 + vt * P
+                        nc.tensor.transpose(xt[:, lo : lo + P], src[:, u * P : (u + 1) * P], ident[:])
+                banks[g].append(xt)
 
         def squares(g):
-            grouped[g] = gpool.tile([P, PAIR * K], BF16, name="grouped", tag="grouped", align_bytes=64)
-            nc.scalar.activation(
-                out=grouped[g][:].rearrange("p (c u e) -> p c u e", u=2, e=2),
-                in_=banks[g][:].bitcast(BF16).rearrange("p (u c e) -> p c u e", u=2, e=2),
-                func=ACT.Square,
-            )
+            grp = gpool.tile([P, GROUPS[g] * K], BF16, name="grouped", tag="grouped", align_bytes=64)
+            for h in range(GROUPS[g] // 2):
+                nc.scalar.activation(
+                    out=grp[:, h * 1024 : (h + 1) * 1024].rearrange("p (c u e) -> p c u e", u=2, e=2),
+                    in_=banks[g][h][:].bitcast(BF16).rearrange("p (u c e) -> p c u e", u=2, e=2),
+                    func=ACT.Square,
+                )
+            grouped[g] = grp
+
+        def squares_on_vector(g):
+            pairs = consts.tile([P, GROUPS[g] * K], BF16, name="pairs")
+            grp = gpool.tile([P, GROUPS[g] * K], BF16, name="grouped", tag="grouped", align_bytes=64)
+            for h in range(GROUPS[g] // 2):
+                nc.vector.tensor_copy(
+                    out=pairs[:].bitcast(F32)[:, h * 512 : (h + 1) * 512].rearrange("p (c u) -> p c u", u=2),
+                    in_=banks[g][h][:].rearrange("p (u c) -> p c u", u=2),
+                )
+            nc.vector.tensor_tensor(out=grp[:], in0=pairs[:], in1=pairs[:], op=ALU.mult)
+            grouped[g] = grp
 
         def quantise(g):
-            codes[g] = gpool.tile([P, PAIR * P], U32, name="codes", tag="codes", align_bytes=64)
-            scales[g] = gpool.tile([P, PAIR * P], U8, name="scales", tag="scales", align_bytes=64)
-            nc.vector.quantize_mx(out=codes[g][:].bitcast(FP8X4), scales=scales[g][:], in_=grouped[g][:])
+            cd = gpool.tile([P, GROUPS[g] * P], U32, name="codes", tag="codes", align_bytes=64)
+            sc = gpool.tile([P, GROUPS[g] * P], U8, name="scales", tag="scales", align_bytes=64)
+            nc.vector.quantize_mx(out=cd[:].bitcast(FP8X4), scales=sc[:], in_=grouped[g][:])
+            codes[g] = cd
+            scales[g] = sc
 
         def multiply(g):
-            b = PAIR * g // TILES
-            for j in range(PAIR):
-                accs[PAIR * g + j] = psum.tile([P, C], F32, name="acc", tag="acc")
+            b = FIRST[g] // TILES
+            accs[g] = []
+            for j in range(GROUPS[g]):
+                acc = psum.tile([P, C], F32, name="acc", tag="acc")
                 nc.tensor.matmul_mx(
-                    out=accs[PAIR * g + j][:],
+                    out=acc[:],
                     lhsT=codes[g][:, j * P : (j + 1) * P].bitcast(FP8X4),
                     lhsT_scale=scales[g][:, j * P : (j + 1) * P],
                     rhs=coef_codes[b][:].bitcast(FP8X4),
@@ -146,52 +157,51 @@ def tile_hks_t_kernel(tc, evals, evecs, count, out):
                     start=True,
                     stop=True,
                 )
+                accs[g].append(acc)
 
-        def copy_out(i, on_scalar):
-            s = STORE_OF[i]
-            if i == STORE_FIRST[s]:
-                stages[s] = spool.tile([P, STORES[s] * C], F32, name="stage", tag="stage")
-            lo = (i - STORE_FIRST[s]) * C
-            if on_scalar:
-                nc.scalar.copy(out=stages[s][:, lo : lo + C], in_=accs[i][:])
-            else:
-                nc.vector.tensor_copy(out=stages[s][:, lo : lo + C], in_=accs[i][:])
+        stages = {}
 
-        def store_if_full(i):
-            s = STORE_OF[i]
-            if i + 1 == STORE_FIRST[s] + STORES[s]:
-                b = i // TILES
-                t0 = STORE_FIRST[s] % TILES
-                dram = out[b].rearrange("(p t) c -> p (t c)", t=TILES)
-                nc.sync.dma_start(out=dram[:, t0 * C : (t0 + STORES[s]) * C], in_=stages[s][:])
+        def vector_copies(g):
+            stage = spool.tile([P, GROUPS[g] * C], F32, name="stage", tag="stage")
+            for j in range(GROUPS[g] - SCALAR_COPIES[g]):
+                nc.vector.tensor_copy(out=stage[:, j * C : (j + 1) * C], in_=accs[g][j][:])
+            stages[g] = stage
+
+        def scalar_copies_and_store(g):
+            b = FIRST[g] // TILES
+            t0 = FIRST[g] % TILES
+            stage = stages[g]
+            for j in range(GROUPS[g] - SCALAR_COPIES[g], GROUPS[g]):
+                nc.scalar.copy(out=stage[:, j * C : (j + 1) * C], in_=accs[g][j][:])
+            dram = out[b].rearrange("(p t) c -> p (t c)", t=TILES)
+            nc.sync.dma_start(out=dram[:, t0 * C : (t0 + GROUPS[g]) * C], in_=stage[:])
 
         coef_args(0)
         coef_args(1)
-        for g in range(T_AHEAD):
-            transposes(g)
+        transposes(0)
+        transposes(1)
         squares(0)
         coef_exp(0)
-        squares(1)
-        for g in range(STEPS + 1):
-            if g < STEPS:
+        quantise(0)
+        squares_on_vector(1)
+        coef_quant(0)
+        transposes(2)
+        transposes(3)
+        squares(2)
+        for g in range(NG + 1):
+            if 0 < g < NG:
                 quantise(g)
-            if g == 0:
-                coef_quant(0)
-            if g + T_AHEAD < STEPS:
-                transposes(g + T_AHEAD)
+            if g > 0 and g + 3 < NG:
+                transposes(g + 3)
             if g > 0:
-                copy_out(PAIR * (g - 1), False)
-                if not scalar_copies_second(g - 1):
-                    copy_out(PAIR * (g - 1) + 1, False)
+                vector_copies(g - 1)
             if g == QUANT1_AT:
                 coef_quant(1)
-            if g + SQ_AHEAD < STEPS:
-                squares(g + SQ_AHEAD)
+            if g > 0 and g + 2 < NG:
+                squares(g + 2)
             if g > 0:
-                if scalar_copies_second(g - 1):
-                    copy_out(PAIR * (g - 1) + 1, True)
-                store_if_full(PAIR * (g - 1) + 1)
-            if g == EXP1_AT:
+                scalar_copies_and_store(g - 1)
+            if g == EXP1_AFTER:
                 coef_exp(1)
-            if g < STEPS:
+            if g < NG:
                 multiply(g)

@@ -12,19 +12,31 @@ ACT = mybir.ActivationFunctionType
 ALU = mybir.AluOpType
 
 P = 128
+PACK = 4
 B, V, K, C = 2, 4096, 512, 512
 TILES = V // P
+PAIRS = K // 2
+HALVES = PAIRS // P
+BANK = 512
+PER_BANK = BANK // PAIRS
+
+FLOPS = 2 * B * V * K * C
+
 GROUPS = [4] * 15 + [2, 2]
 NG = len(GROUPS)
 FIRST = [sum(GROUPS[:g]) for g in range(NG)]
 
-FLOPS = 2 * B * V * K * C
-
 LOADS = [(0, 0, 2), (0, 2, 2), (0, 4, 4), (0, 8, 8), (0, 16, 16), (1, 0, 32)]
-STAGE_BUFS = 10
-SCALAR_COPIES = [0, 0, 1, 0, 1, 0, 1, 0, 1, 0, 1, 0, 1, 1, 2, 1, 1]
-EXP1_AFTER = 3
-QUANT1_AT = 5
+
+STORES = [8, 8] + [4] * 11 + [2, 2]
+STORE_FIRST = [sum(STORES[:s]) for s in range(len(STORES))]
+STORE_OF = [s for s in range(len(STORES)) for i in range(STORES[s])]
+STAGE_BUFS = 8
+
+SCALAR_COPIES = [0, 0, 0, 0, 0, 0, 1, 0, 1, 0, 1, 0, 1, 1, 2, 1, 1]
+
+EXP1_STEP = 3
+QUANT1_STEP = 5
 
 
 def tile_hks_t_kernel(tc, evals, evecs, count, out):
@@ -39,20 +51,20 @@ def tile_hks_t_kernel(tc, evals, evecs, count, out):
         psum = ctx.enter_context(tc.psum_pool(name="psum", bufs=4))
         ctx.enter_context(tc.manual_schedule())
 
-        ev = consts.tile([P, 4 * B], BF16, name="ev")
+        ev = consts.tile([P, PACK * B], BF16, name="ev")
         with nc.allow_non_contiguous_dma(reason="evals: two neighbouring values to a partition"):
             nc.sync.dma_start(
-                out=ev[:].rearrange("p (b u e) -> p b u e", b=B, u=2, e=2),
-                in_=evals.rearrange("b (u p e) -> p b u e", u=2, p=P, e=2),
+                out=ev[:].rearrange("p (b u e) -> p b u e", b=B, u=HALVES, e=2),
+                in_=evals.rearrange("b (u p e) -> p b u e", u=HALVES, p=P, e=2),
             )
-        words = {}
+        pairs = {}
         for b, t0, n in LOADS:
             x = xpool.tile([P, n * K], BF16, name="x_%d_%d" % (b, t0))
-            src = evecs[b].rearrange("(p t) k -> p (t k)", t=TILES)
-            nc.sync.dma_start(out=x[:], in_=src[:, t0 * K : (t0 + n) * K])
-            xw = x[:].bitcast(F32)
+            x_rows = evecs[b].rearrange("(p t) k -> p (t k)", t=TILES)
+            nc.sync.dma_start(out=x[:], in_=x_rows[:, t0 * K : (t0 + n) * K])
+            x_pairs = x[:].bitcast(F32)
             for j in range(n):
-                words[b * TILES + t0 + j] = xw[:, j * (K // 2) : (j + 1) * (K // 2)]
+                pairs[b * TILES + t0 + j] = x_pairs[:, j * PAIRS : (j + 1) * PAIRS]
 
         ident = consts.tile([P, P], F32, name="ident")
         make_identity(nc, ident[:])
@@ -61,147 +73,136 @@ def tile_hks_t_kernel(tc, evals, evecs, count, out):
         nc.vector.memset(powers[:, 0:1], 1.0)
         warm = consts.tile([P, 1], F32, name="warm")
         nc.scalar.activation(out=warm[:], in_=powers[:, 0:1], func=ACT.Exp)
-        n = 1
-        while n < C:
+        filled = 1
+        while filled < C:
             nc.vector.tensor_scalar(
-                out=powers[:, n : 2 * n],
-                in0=powers[:, 0:n],
-                scalar1=10.0 ** (2.0 * n / (C - 1)),
+                out=powers[:, filled : 2 * filled],
+                in0=powers[:, 0:filled],
+                scalar1=10.0 ** (2.0 * filled / (C - 1)),
                 scalar2=None,
                 op0=ALU.mult,
             )
-            n *= 2
+            filled *= 2
 
-        args = {}
+        exp_args = {}
+        coefs = {}
         coef_codes = {}
-        coef_scales = {}
+        coef_scale_bytes = {}
 
-        def coef_args(b):
-            a = consts.tile([P, 4 * C], F32, name="arg%d" % b)
+        def coef_exp_args(b):
+            exp_args[b] = consts.tile([P, PACK * C], F32, name="arg%d" % b)
             nc.vector.tensor_tensor(
-                out=a[:].rearrange("p (c t) -> p c t", t=4),
-                in0=powers[:].unsqueeze(2).to_broadcast([P, C, 4]),
-                in1=ev[:, 4 * b : 4 * b + 4].unsqueeze(1).to_broadcast([P, C, 4]),
+                out=exp_args[b][:].rearrange("p (c t) -> p c t", t=PACK),
+                in0=powers[:].unsqueeze(2).to_broadcast([P, C, PACK]),
+                in1=ev[:, PACK * b : PACK * (b + 1)].unsqueeze(1).to_broadcast([P, C, PACK]),
                 op=ALU.mult,
             )
-            args[b] = a
 
         def coef_exp(b):
-            cf = consts.tile([P, 4 * C], BF16, name="cf%d" % b, align_bytes=64)
-            nc.scalar.activation(out=cf[:], in_=args[b][:], func=ACT.Exp, scale=-0.01)
-            args[b] = cf
+            coefs[b] = consts.tile([P, PACK * C], BF16, name="cf%d" % b, align_bytes=64)
+            nc.scalar.activation(out=coefs[b][:], in_=exp_args[b][:], func=ACT.Exp, scale=-0.01)
 
-        def coef_quant(b):
-            cc = consts.tile([P, C], U32, name="cc%d" % b, align_bytes=64)
-            cs = consts.tile([P, C], U8, name="cs%d" % b, align_bytes=64)
-            nc.vector.quantize_mx(out=cc[:].bitcast(FP8X4), scales=cs[:], in_=args[b][:])
-            coef_codes[b] = cc
-            coef_scales[b] = cs
+        def coef_quantise(b):
+            coef_codes[b] = consts.tile([P, C], U32, name="cc%d" % b, align_bytes=64)
+            coef_scale_bytes[b] = consts.tile([P, C], U8, name="cs%d" % b, align_bytes=64)
+            nc.vector.quantize_mx(
+                out=coef_codes[b][:].bitcast(FP8X4), scales=coef_scale_bytes[b][:], in_=coefs[b][:]
+            )
 
         banks = {}
-        grouped = {}
+        squared = {}
         codes = {}
-        scales = {}
-        accs = {}
+        scale_bytes = {}
+        sums = {}
+        stages = {}
 
         def transposes(g):
             banks[g] = []
-            for h in range(GROUPS[g] // 2):
-                xt = psum.tile([P, 512], F32, name="xt", tag="xt")
-                for vt in range(2):
-                    src = words[FIRST[g] + 2 * h + vt]
-                    for u in range(2):
-                        lo = u * 256 + vt * P
-                        nc.tensor.transpose(xt[:, lo : lo + P], src[:, u * P : (u + 1) * P], ident[:])
-                banks[g].append(xt)
+            for h in range(GROUPS[g] // PER_BANK):
+                bank = psum.tile([P, BANK], F32, name="xt", tag="xt")
+                for i in range(PER_BANK):
+                    tile_pairs = pairs[FIRST[g] + PER_BANK * h + i]
+                    for u in range(HALVES):
+                        lo = (u * PER_BANK + i) * P
+                        nc.tensor.transpose(bank[:, lo : lo + P], tile_pairs[:, u * P : (u + 1) * P], ident[:])
+                banks[g].append(bank)
 
         def squares(g):
-            grp = gpool.tile([P, GROUPS[g] * K], BF16, name="grouped", tag="grouped", align_bytes=64)
-            for h in range(GROUPS[g] // 2):
+            squared[g] = gpool.tile([P, GROUPS[g] * K], BF16, name="grouped", tag="grouped", align_bytes=64)
+            for h in range(GROUPS[g] // PER_BANK):
                 nc.scalar.activation(
-                    out=grp[:, h * 1024 : (h + 1) * 1024].rearrange("p (c u e) -> p c u e", u=2, e=2),
-                    in_=banks[g][h][:].bitcast(BF16).rearrange("p (u c e) -> p c u e", u=2, e=2),
+                    out=squared[g][:, h * PER_BANK * K : (h + 1) * PER_BANK * K].rearrange(
+                        "p (r u e) -> p r u e", u=HALVES, e=2
+                    ),
+                    in_=banks[g][h][:].bitcast(BF16).rearrange("p (u r e) -> p r u e", u=HALVES, e=2),
                     func=ACT.Square,
                 )
-            grouped[g] = grp
-
-        def squares_on_vector(g):
-            pairs = consts.tile([P, GROUPS[g] * K], BF16, name="pairs")
-            grp = gpool.tile([P, GROUPS[g] * K], BF16, name="grouped", tag="grouped", align_bytes=64)
-            for h in range(GROUPS[g] // 2):
-                nc.vector.tensor_copy(
-                    out=pairs[:].bitcast(F32)[:, h * 512 : (h + 1) * 512].rearrange("p (c u) -> p c u", u=2),
-                    in_=banks[g][h][:].rearrange("p (u c) -> p c u", u=2),
-                )
-            nc.vector.tensor_tensor(out=grp[:], in0=pairs[:], in1=pairs[:], op=ALU.mult)
-            grouped[g] = grp
 
         def quantise(g):
-            cd = gpool.tile([P, GROUPS[g] * P], U32, name="codes", tag="codes", align_bytes=64)
-            sc = gpool.tile([P, GROUPS[g] * P], U8, name="scales", tag="scales", align_bytes=64)
-            nc.vector.quantize_mx(out=cd[:].bitcast(FP8X4), scales=sc[:], in_=grouped[g][:])
-            codes[g] = cd
-            scales[g] = sc
+            codes[g] = gpool.tile([P, GROUPS[g] * P], U32, name="codes", tag="codes", align_bytes=64)
+            scale_bytes[g] = gpool.tile([P, GROUPS[g] * P], U8, name="scales", tag="scales", align_bytes=64)
+            nc.vector.quantize_mx(out=codes[g][:].bitcast(FP8X4), scales=scale_bytes[g][:], in_=squared[g][:])
 
         def multiply(g):
             b = FIRST[g] // TILES
-            accs[g] = []
+            sums[g] = []
             for j in range(GROUPS[g]):
                 acc = psum.tile([P, C], F32, name="acc", tag="acc")
                 nc.tensor.matmul_mx(
                     out=acc[:],
                     lhsT=codes[g][:, j * P : (j + 1) * P].bitcast(FP8X4),
-                    lhsT_scale=scales[g][:, j * P : (j + 1) * P],
+                    lhsT_scale=scale_bytes[g][:, j * P : (j + 1) * P],
                     rhs=coef_codes[b][:].bitcast(FP8X4),
-                    rhs_scale=coef_scales[b][:],
+                    rhs_scale=coef_scale_bytes[b][:],
                     start=True,
                     stop=True,
                 )
-                accs[g].append(acc)
-
-        stages = {}
+                sums[g].append(acc)
 
         def vector_copies(g):
-            stage = spool.tile([P, GROUPS[g] * C], F32, name="stage", tag="stage")
+            s = STORE_OF[FIRST[g]]
+            if FIRST[g] == STORE_FIRST[s]:
+                if STORES[s] > 4:
+                    stages[s] = spool.tile([P, STORES[s] * C], F32, name="stage8", tag="stage8", bufs=2)
+                else:
+                    stages[s] = spool.tile([P, STORES[s] * C], F32, name="stage", tag="stage")
             for j in range(GROUPS[g] - SCALAR_COPIES[g]):
-                nc.vector.tensor_copy(out=stage[:, j * C : (j + 1) * C], in_=accs[g][j][:])
-            stages[g] = stage
+                lo = (FIRST[g] - STORE_FIRST[s] + j) * C
+                nc.vector.tensor_copy(out=stages[s][:, lo : lo + C], in_=sums[g][j][:])
 
         def scalar_copies_and_store(g):
-            b = FIRST[g] // TILES
-            t0 = FIRST[g] % TILES
-            stage = stages[g]
+            s = STORE_OF[FIRST[g]]
             for j in range(GROUPS[g] - SCALAR_COPIES[g], GROUPS[g]):
-                nc.scalar.copy(out=stage[:, j * C : (j + 1) * C], in_=accs[g][j][:])
-            dram = out[b].rearrange("(p t) c -> p (t c)", t=TILES)
-            nc.sync.dma_start(out=dram[:, t0 * C : (t0 + GROUPS[g]) * C], in_=stage[:])
+                lo = (FIRST[g] - STORE_FIRST[s] + j) * C
+                nc.scalar.copy(out=stages[s][:, lo : lo + C], in_=sums[g][j][:])
+            if FIRST[g] + GROUPS[g] == STORE_FIRST[s] + STORES[s]:
+                b = STORE_FIRST[s] // TILES
+                t0 = STORE_FIRST[s] % TILES
+                out_rows = out[b].rearrange("(p t) c -> p (t c)", t=TILES)
+                nc.sync.dma_start(out=out_rows[:, t0 * C : (t0 + STORES[s]) * C], in_=stages[s][:])
 
-        coef_args(0)
-        coef_args(1)
+        coef_exp_args(0)
+        coef_exp_args(1)
         transposes(0)
         transposes(1)
         squares(0)
         coef_exp(0)
-        quantise(0)
-        squares_on_vector(1)
-        coef_quant(0)
-        transposes(2)
-        transposes(3)
-        squares(2)
-        for g in range(NG + 1):
-            if 0 < g < NG:
-                quantise(g)
-            if g > 0 and g + 3 < NG:
-                transposes(g + 3)
+        for g in range(NG):
+            quantise(g)
+            if g == 0:
+                coef_quantise(0)
+            if g + 2 < NG:
+                transposes(g + 2)
             if g > 0:
                 vector_copies(g - 1)
-            if g == QUANT1_AT:
-                coef_quant(1)
-            if g > 0 and g + 2 < NG:
-                squares(g + 2)
+            if g == QUANT1_STEP:
+                coef_quantise(1)
+            if g + 1 < NG:
+                squares(g + 1)
             if g > 0:
                 scalar_copies_and_store(g - 1)
-            if g == EXP1_AFTER:
+            if g == EXP1_STEP:
                 coef_exp(1)
-            if g < NG:
-                multiply(g)
+            multiply(g)
+        vector_copies(NG - 1)
+        scalar_copies_and_store(NG - 1)

from contextlib import ExitStack

import concourse.mybir as mybir
from concourse.masks import make_identity

F32 = mybir.dt.float32
BF16 = mybir.dt.bfloat16
U32 = mybir.dt.uint32
U8 = mybir.dt.uint8
FP8X4 = mybir.dt.float8_e4m3fn_x4
ACT = mybir.ActivationFunctionType
ALU = mybir.AluOpType

P = 128
PACK = 4
B, V, K, C = 2, 4096, 512, 512
TILES = V // P
PAIRS = K // 2
HALVES = PAIRS // P
BANK = 512
PER_BANK = BANK // PAIRS

FLOPS = 2 * B * V * K * C

GROUPS = [4] * 15 + [2, 2]
NG = len(GROUPS)
FIRST = [sum(GROUPS[:g]) for g in range(NG)]

LOADS = [(0, 0, 2), (0, 2, 2), (0, 4, 4), (0, 8, 8), (0, 16, 16), (1, 0, 32)]

STORES = [8, 8] + [4] * 11 + [2, 2]
STORE_FIRST = [sum(STORES[:s]) for s in range(len(STORES))]
STORE_OF = [s for s in range(len(STORES)) for i in range(STORES[s])]
STAGE_BUFS = 8

SCALAR_COPIES = [0, 0, 0, 0, 0, 0, 1, 0, 1, 0, 1, 0, 1, 1, 2, 1, 1]

EXP1_STEP = 3
QUANT1_STEP = 5


def tile_hks_t_kernel(tc, evals, evecs, count, out):
    nc = tc.nc
    assert tuple(evecs.shape) == (B, V, K) and count == C

    with ExitStack() as ctx:
        consts = ctx.enter_context(tc.tile_pool(name="consts", bufs=1))
        xpool = ctx.enter_context(tc.tile_pool(name="xpool", bufs=1))
        gpool = ctx.enter_context(tc.tile_pool(name="gpool", bufs=3))
        spool = ctx.enter_context(tc.tile_pool(name="spool", bufs=STAGE_BUFS))
        psum = ctx.enter_context(tc.psum_pool(name="psum", bufs=4))
        ctx.enter_context(tc.manual_schedule())

        ev = consts.tile([P, PACK * B], BF16, name="ev")
        with nc.allow_non_contiguous_dma(reason="evals: two neighbouring values to a partition"):
            nc.sync.dma_start(
                out=ev[:].rearrange("p (b u e) -> p b u e", b=B, u=HALVES, e=2),
                in_=evals.rearrange("b (u p e) -> p b u e", u=HALVES, p=P, e=2),
            )
        pairs = {}
        for b, t0, n in LOADS:
            x = xpool.tile([P, n * K], BF16, name="x_%d_%d" % (b, t0))
            x_rows = evecs[b].rearrange("(p t) k -> p (t k)", t=TILES)
            nc.sync.dma_start(out=x[:], in_=x_rows[:, t0 * K : (t0 + n) * K])
            x_pairs = x[:].bitcast(F32)
            for j in range(n):
                pairs[b * TILES + t0 + j] = x_pairs[:, j * PAIRS : (j + 1) * PAIRS]

        ident = consts.tile([P, P], F32, name="ident")
        make_identity(nc, ident[:])

        powers = consts.tile([P, C], F32, name="powers")
        nc.vector.memset(powers[:, 0:1], 1.0)
        warm = consts.tile([P, 1], F32, name="warm")
        nc.scalar.activation(out=warm[:], in_=powers[:, 0:1], func=ACT.Exp)
        filled = 1
        while filled < C:
            nc.vector.tensor_scalar(
                out=powers[:, filled : 2 * filled],
                in0=powers[:, 0:filled],
                scalar1=10.0 ** (2.0 * filled / (C - 1)),
                scalar2=None,
                op0=ALU.mult,
            )
            filled *= 2

        exp_args = {}
        coefs = {}
        coef_codes = {}
        coef_scale_bytes = {}

        def coef_exp_args(b):
            exp_args[b] = consts.tile([P, PACK * C], F32, name="arg%d" % b)
            nc.vector.tensor_tensor(
                out=exp_args[b][:].rearrange("p (c t) -> p c t", t=PACK),
                in0=powers[:].unsqueeze(2).to_broadcast([P, C, PACK]),
                in1=ev[:, PACK * b : PACK * (b + 1)].unsqueeze(1).to_broadcast([P, C, PACK]),
                op=ALU.mult,
            )

        def coef_exp(b):
            coefs[b] = consts.tile([P, PACK * C], BF16, name="cf%d" % b, align_bytes=64)
            nc.scalar.activation(out=coefs[b][:], in_=exp_args[b][:], func=ACT.Exp, scale=-0.01)

        def coef_quantise(b):
            coef_codes[b] = consts.tile([P, C], U32, name="cc%d" % b, align_bytes=64)
            coef_scale_bytes[b] = consts.tile([P, C], U8, name="cs%d" % b, align_bytes=64)
            nc.vector.quantize_mx(
                out=coef_codes[b][:].bitcast(FP8X4), scales=coef_scale_bytes[b][:], in_=coefs[b][:]
            )

        banks = {}
        squared = {}
        codes = {}
        scale_bytes = {}
        sums = {}
        stages = {}

        def transposes(g):
            banks[g] = []
            for h in range(GROUPS[g] // PER_BANK):
                bank = psum.tile([P, BANK], F32, name="xt", tag="xt")
                for i in range(PER_BANK):
                    tile_pairs = pairs[FIRST[g] + PER_BANK * h + i]
                    for u in range(HALVES):
                        lo = (u * PER_BANK + i) * P
                        nc.tensor.transpose(bank[:, lo : lo + P], tile_pairs[:, u * P : (u + 1) * P], ident[:])
                banks[g].append(bank)

        def squares(g):
            squared[g] = gpool.tile([P, GROUPS[g] * K], BF16, name="grouped", tag="grouped", align_bytes=64)
            for h in range(GROUPS[g] // PER_BANK):
                nc.scalar.activation(
                    out=squared[g][:, h * PER_BANK * K : (h + 1) * PER_BANK * K].rearrange(
                        "p (r u e) -> p r u e", u=HALVES, e=2
                    ),
                    in_=banks[g][h][:].bitcast(BF16).rearrange("p (u r e) -> p r u e", u=HALVES, e=2),
                    func=ACT.Square,
                )

        def quantise(g):
            codes[g] = gpool.tile([P, GROUPS[g] * P], U32, name="codes", tag="codes", align_bytes=64)
            scale_bytes[g] = gpool.tile([P, GROUPS[g] * P], U8, name="scales", tag="scales", align_bytes=64)
            nc.vector.quantize_mx(out=codes[g][:].bitcast(FP8X4), scales=scale_bytes[g][:], in_=squared[g][:])

        def multiply(g):
            b = FIRST[g] // TILES
            sums[g] = []
            for j in range(GROUPS[g]):
                acc = psum.tile([P, C], F32, name="acc", tag="acc")
                nc.tensor.matmul_mx(
                    out=acc[:],
                    lhsT=codes[g][:, j * P : (j + 1) * P].bitcast(FP8X4),
                    lhsT_scale=scale_bytes[g][:, j * P : (j + 1) * P],
                    rhs=coef_codes[b][:].bitcast(FP8X4),
                    rhs_scale=coef_scale_bytes[b][:],
                    start=True,
                    stop=True,
                )
                sums[g].append(acc)

        def vector_copies(g):
            s = STORE_OF[FIRST[g]]
            if FIRST[g] == STORE_FIRST[s]:
                if STORES[s] > 4:
                    stages[s] = spool.tile([P, STORES[s] * C], F32, name="stage8", tag="stage8", bufs=2)
                else:
                    stages[s] = spool.tile([P, STORES[s] * C], F32, name="stage", tag="stage")
            for j in range(GROUPS[g] - SCALAR_COPIES[g]):
                lo = (FIRST[g] - STORE_FIRST[s] + j) * C
                nc.vector.tensor_copy(out=stages[s][:, lo : lo + C], in_=sums[g][j][:])

        def scalar_copies_and_store(g):
            s = STORE_OF[FIRST[g]]
            for j in range(GROUPS[g] - SCALAR_COPIES[g], GROUPS[g]):
                lo = (FIRST[g] - STORE_FIRST[s] + j) * C
                nc.scalar.copy(out=stages[s][:, lo : lo + C], in_=sums[g][j][:])
            if FIRST[g] + GROUPS[g] == STORE_FIRST[s] + STORES[s]:
                b = STORE_FIRST[s] // TILES
                t0 = STORE_FIRST[s] % TILES
                out_rows = out[b].rearrange("(p t) c -> p (t c)", t=TILES)
                nc.sync.dma_start(out=out_rows[:, t0 * C : (t0 + STORES[s]) * C], in_=stages[s][:])

        coef_exp_args(0)
        coef_exp_args(1)
        transposes(0)
        transposes(1)
        squares(0)
        coef_exp(0)
        for g in range(NG):
            quantise(g)
            if g == 0:
                coef_quantise(0)
            if g + 2 < NG:
                transposes(g + 2)
            if g > 0:
                vector_copies(g - 1)
            if g == QUANT1_STEP:
                coef_quantise(1)
            if g + 1 < NG:
                squares(g + 1)
            if g > 0:
                scalar_copies_and_store(g - 1)
            if g == EXP1_STEP:
                coef_exp(1)
            multiply(g)
        vector_copies(NG - 1)
        scalar_copies_and_store(NG - 1)
